import numpy as np
import ml_dtypes

BF16 = ml_dtypes.bfloat16


def bf(x):
    return np.asarray(x, np.float32).astype(BF16)


def f32(x):
    return np.asarray(x, np.float32)


def f64(x):
    return np.asarray(x).astype(np.float64)


def striped(idx):
    return np.tile(idx.reshape(-1, 16).T, (8, 1))


C, HC, S, N = 256, 128, 2048, 512


def gelu_tanh(v):
    return 0.5 * v * (1.0 + np.tanh(np.sqrt(2.0 / np.pi) * (v + 0.044715 * v**3)))


def arc_table():
    div = np.exp(np.arange(HC, dtype=np.float64) * (-np.log(10000.0) / HC))
    return div[:, None] * np.arange(N, dtype=np.float64)[None, :]


def setup_inputs():
    arc = arc_table()
    return {
        "emb": f32(0.1 * np.random.standard_normal((C, S))),
        "seq_dt": f32(np.random.uniform(0.0, 1.0, (1, N))),
        "wt": f32(np.random.uniform(-1.5, 1.5, (HC, 1))),
        "sin_arc": f32(np.sin(arc)),
        "cos_arc": f32(np.cos(arc)),
        "ws": bf(np.random.standard_normal((C, C)) / np.sqrt(C)),
        "bs": f32(0.1 * np.random.standard_normal((C, 1))),
        "offs": striped(np.random.permutation(np.tile(np.arange(S), 2))[:N]),
    }


def reference(emb, seq_dt, wt, sin_arc, cos_arc, ws, bs, offs):
    idx = offs[:16].T.reshape(-1)
    phi = f64(wt) * f64(seq_dt)
    sp, cp = np.sin(phi), np.cos(phi)
    sa, ca = f64(sin_arc), f64(cos_arc)
    pe = np.concatenate([sa * cp + ca * sp, ca * cp - sa * sp], axis=0)
    x = np.sqrt(C) * f64(emb)[:, idx] + pe
    return gelu_tanh(f64(ws).T @ x + f64(bs))

@@ -1,0 +1,91 @@
+import math
+
+import concourse.mybir as mybir
+
+F32 = mybir.dt.float32
+BF16 = mybir.dt.bfloat16
+U16 = mybir.dt.uint16
+FUNC = mybir.ActivationFunctionType
+ALU = mybir.AluOpType
+
+P = 128
+C = 256
+S = 2048
+N = 512
+BLOCKS = C // P
+SCALE = 16.0
+
+FLOPS = 2 * C * C * N
+
+
+def tile_sahp_kernel(tc, emb, seq_dt, wt, sin_arc, cos_arc, ws, bs, offs, out):
+    nc = tc.nc
+    with (
+        tc.tile_pool(name="held", bufs=1) as held,
+        tc.psum_pool(name="psum", bufs=1) as psum,
+    ):
+        offsets = held.tile([P, N // 16], U16, name="offsets")
+        nc.sync.dma_start(offsets[:], offs)
+
+        dt_all = held.tile([P, N], F32, name="dt_all")
+        nc.scalar.dma_start(dt_all[:], seq_dt.broadcast_to([P, N]))
+        wt_col = held.tile([P, 1], F32, name="wt_col")
+        nc.scalar.dma_start(wt_col[:], wt)
+
+        sin_a = held.tile([P, N], F32, name="sin_a")
+        nc.sync.dma_start(sin_a[:], sin_arc)
+        cos_a = held.tile([P, N], F32, name="cos_a")
+        nc.sync.dma_start(cos_a[:], cos_arc)
+
+        table = []
+        for b in range(BLOCKS):
+            table_b = held.tile([P, S], F32, name=f"table{b}")
+            nc.sync.dma_start(table_b[:], emb[b * P : (b + 1) * P, :])
+            table.append(table_b)
+
+        weights = held.tile([P, BLOCKS, C], BF16, name="weights")
+        nc.sync.dma_start(weights[:], ws.rearrange("(kb p) m -> p kb m", p=P))
+        bias = held.tile([P, BLOCKS], F32, name="bias")
+        with nc.allow_non_contiguous_dma(reason="256 biases, one to a partition"):
+            nc.scalar.dma_start(bias[:], bs.rearrange("(mb p) o -> p (mb o)", p=P))
+
+        sin_p = held.tile([P, N], F32, name="sin_p")
+        nc.scalar.activation(sin_p[:], dt_all[:], FUNC.Sin, scale=wt_col[:, 0:1])
+        cos_p = held.tile([P, N], F32, name="cos_p")
+        nc.scalar.activation(cos_p[:], dt_all[:], FUNC.Sin, bias=math.pi / 2, scale=wt_col[:, 0:1])
+
+        def scaled_product(name, arc, shift):
+            prod = held.tile([P, N], F32, name=name)
+            nc.vector.scalar_tensor_tensor(prod[:], arc[:], 1.0 / SCALE, shift[:], ALU.mult, ALU.mult)
+            return prod
+
+        sc = scaled_product("sc", sin_a, cos_p)
+        cs = scaled_product("cs", cos_a, sin_p)
+        cc = scaled_product("cc", cos_a, cos_p)
+        ss = scaled_product("ss", sin_a, sin_p)
+        pe = [held.tile([P, N], F32, name=f"pe{b}") for b in range(BLOCKS)]
+        nc.vector.tensor_tensor(pe[0][:], sc[:], cs[:], ALU.add)
+        nc.vector.tensor_tensor(pe[1][:], cc[:], ss[:], ALU.subtract)
+
+        x = []
+        for b in range(BLOCKS):
+            picked = held.tile([P, N], F32, name=f"picked{b}")
+            nc.vector.tensor_tensor(picked[:], table[b][:].indirect(offsets[:]), pe[b][:], ALU.add)
+            x_b = held.tile([P, N], BF16, name=f"x{b}")
+            nc.vector.tensor_scalar(x_b[:], picked[:], SCALE, None, ALU.mult)
+            x.append(x_b)
+
+        acc = [psum.tile([P, N], F32, name=f"acc{mb}") for mb in range(BLOCKS)]
+        for kb in range(BLOCKS):
+            for mb in range(BLOCKS):
+                nc.tensor.matmul(
+                    acc[mb][:],
+                    weights[:, kb, mb * P : (mb + 1) * P],
+                    x[kb][:],
+                    start=(kb == 0),
+                    stop=(kb == BLOCKS - 1),
+                )
+        for mb in range(BLOCKS):
+            y = held.tile([P, N], F32, name=f"y{mb}")
+            nc.scalar.activation(y[:], acc[mb][:], FUNC.Gelu_apprx_tanh, bias=bias[:, mb : mb + 1])
+            nc.sync.dma_start(out[mb * P : (mb + 1) * P, :], y[:])

@@ -28,7 +28,7 @@ def tile_sahp_kernel(tc, emb, seq_dt, wt, sin_arc, cos_arc, ws, bs, offs, out):
         nc.sync.dma_start(offsets[:], offs)
 
         dt_all = held.tile([P, N], F32, name="dt_all")
-        nc.scalar.dma_start(dt_all[:], seq_dt.broadcast_to([P, N]))
+        nc.sync.dma_start(dt_all[:], seq_dt.broadcast_to([P, N]))
         wt_col = held.tile([P, 1], F32, name="wt_col")
         nc.scalar.dma_start(wt_col[:], wt)
 
@@ -49,10 +49,15 @@ def tile_sahp_kernel(tc, emb, seq_dt, wt, sin_arc, cos_arc, ws, bs, offs, out):
         with nc.allow_non_contiguous_dma(reason="256 biases, one to a partition"):
             nc.scalar.dma_start(bias[:], bs.rearrange("(mb p) o -> p (mb o)", p=P))
 
-        sin_p = held.tile([P, N], F32, name="sin_p")
-        nc.scalar.activation(sin_p[:], dt_all[:], FUNC.Sin, scale=wt_col[:, 0:1])
+        zero = held.tile([P, 1], F32, name="zero")
+        nc.vector.memset(zero[:], 0.0)
+        scratch = held.tile([P, 2], F32, name="scratch")
+        nc.scalar.activation(scratch[:, 0:1], zero[:], FUNC.Sin)
         cos_p = held.tile([P, N], F32, name="cos_p")
         nc.scalar.activation(cos_p[:], dt_all[:], FUNC.Sin, bias=math.pi / 2, scale=wt_col[:, 0:1])
+        sin_p = held.tile([P, N], F32, name="sin_p")
+        nc.scalar.activation(sin_p[:], dt_all[:], FUNC.Sin, scale=wt_col[:, 0:1])
+        nc.scalar.activation(scratch[:, 1:2], sin_p[:, 0:1], FUNC.Gelu_apprx_tanh)
 
         def scaled_product(name, arc, shift):
             prod = held.tile([P, N], F32, name=name)
@@ -60,8 +65,8 @@ def tile_sahp_kernel(tc, emb, seq_dt, wt, sin_arc, cos_arc, ws, bs, offs, out):
             return prod
 
         sc = scaled_product("sc", sin_a, cos_p)
-        cs = scaled_product("cs", cos_a, sin_p)
         cc = scaled_product("cc", cos_a, cos_p)
+        cs = scaled_product("cs", cos_a, sin_p)
         ss = scaled_product("ss", sin_a, sin_p)
         pe = [held.tile([P, N], F32, name=f"pe{b}") for b in range(BLOCKS)]
         nc.vector.tensor_tensor(pe[0][:], sc[:], cs[:], ALU.add)
@@ -72,7 +77,10 @@ def tile_sahp_kernel(tc, emb, seq_dt, wt, sin_arc, cos_arc, ws, bs, offs, out):
             picked = held.tile([P, N], F32, name=f"picked{b}")
             nc.vector.tensor_tensor(picked[:], table[b][:].indirect(offsets[:]), pe[b][:], ALU.add)
             x_b = held.tile([P, N], BF16, name=f"x{b}")
-            nc.vector.tensor_scalar(x_b[:], picked[:], SCALE, None, ALU.mult)
+            if b == 0:
+                nc.scalar.activation(x_b[:], picked[:], FUNC.Copy, scale=SCALE)
+            else:
+                nc.vector.tensor_scalar(x_b[:], picked[:], SCALE, None, ALU.mult)
             x.append(x_b)
 
         acc = [psum.tile([P, N], F32, name=f"acc{mb}") for mb in range(BLOCKS)]

@@ -14,6 +14,8 @@ S = 2048
 N = 512
 BLOCKS = C // P
 SCALE = 16.0
+PIECES = 2
+W = N // PIECES
 
 FLOPS = 2 * C * C * N
 
@@ -24,25 +26,21 @@ def tile_sahp_kernel(tc, emb, seq_dt, wt, sin_arc, cos_arc, ws, bs, offs, out):
         tc.tile_pool(name="held", bufs=1) as held,
         tc.psum_pool(name="psum", bufs=1) as psum,
     ):
-        offsets = held.tile([P, N // 16], U16, name="offsets")
-        nc.sync.dma_start(offsets[:], offs)
-
         dt_all = held.tile([P, N], F32, name="dt_all")
         nc.sync.dma_start(dt_all[:], seq_dt.broadcast_to([P, N]))
         wt_col = held.tile([P, 1], F32, name="wt_col")
         nc.scalar.dma_start(wt_col[:], wt)
-
+        offsets = held.tile([P, N // 16], U16, name="offsets")
+        nc.sync.dma_start(offsets[:], offs)
         sin_a = held.tile([P, N], F32, name="sin_a")
         nc.sync.dma_start(sin_a[:], sin_arc)
         cos_a = held.tile([P, N], F32, name="cos_a")
         nc.sync.dma_start(cos_a[:], cos_arc)
-
         table = []
         for b in range(BLOCKS):
             table_b = held.tile([P, S], F32, name=f"table{b}")
             nc.sync.dma_start(table_b[:], emb[b * P : (b + 1) * P, :])
             table.append(table_b)
-
         weights = held.tile([P, BLOCKS, C], BF16, name="weights")
         nc.sync.dma_start(weights[:], ws.rearrange("(kb p) m -> p kb m", p=P))
         bias = held.tile([P, BLOCKS], F32, name="bias")
@@ -64,36 +62,45 @@ def tile_sahp_kernel(tc, emb, seq_dt, wt, sin_arc, cos_arc, ws, bs, offs, out):
             nc.vector.scalar_tensor_tensor(prod[:], arc[:], 1.0 / SCALE, shift[:], ALU.mult, ALU.mult)
             return prod
 
+        pe = [held.tile([P, N], F32, name=f"pe{b}") for b in range(BLOCKS)]
         sc = scaled_product("sc", sin_a, cos_p)
         cc = scaled_product("cc", cos_a, cos_p)
         cs = scaled_product("cs", cos_a, sin_p)
         ss = scaled_product("ss", sin_a, sin_p)
-        pe = [held.tile([P, N], F32, name=f"pe{b}") for b in range(BLOCKS)]
         nc.vector.tensor_tensor(pe[0][:], sc[:], cs[:], ALU.add)
         nc.vector.tensor_tensor(pe[1][:], cc[:], ss[:], ALU.subtract)
 
-        x = []
+        x = {}
         for b in range(BLOCKS):
-            picked = held.tile([P, N], F32, name=f"picked{b}")
-            nc.vector.tensor_tensor(picked[:], table[b][:].indirect(offsets[:]), pe[b][:], ALU.add)
-            x_b = held.tile([P, N], BF16, name=f"x{b}")
-            if b == 0:
-                nc.scalar.activation(x_b[:], picked[:], FUNC.Copy, scale=SCALE)
-            else:
-                nc.vector.tensor_scalar(x_b[:], picked[:], SCALE, None, ALU.mult)
-            x.append(x_b)
-
-        acc = [psum.tile([P, N], F32, name=f"acc{mb}") for mb in range(BLOCKS)]
-        for kb in range(BLOCKS):
-            for mb in range(BLOCKS):
-                nc.tensor.matmul(
-                    acc[mb][:],
-                    weights[:, kb, mb * P : (mb + 1) * P],
-                    x[kb][:],
-                    start=(kb == 0),
-                    stop=(kb == BLOCKS - 1),
+            for h in range(PIECES):
+                picked = held.tile([P, W], F32, name=f"picked{b}_{h}")
+                nc.vector.tensor_tensor(
+                    picked[:],
+                    table[b][:].indirect(offsets[:, h * W // 16 : (h + 1) * W // 16]),
+                    pe[b][:, h * W : (h + 1) * W],
+                    ALU.add,
                 )
-        for mb in range(BLOCKS):
-            y = held.tile([P, N], F32, name=f"y{mb}")
-            nc.scalar.activation(y[:], acc[mb][:], FUNC.Gelu_apprx_tanh, bias=bias[:, mb : mb + 1])
-            nc.sync.dma_start(out[mb * P : (mb + 1) * P, :], y[:])
+                x[b, h] = held.tile([P, W], BF16, name=f"x{b}_{h}")
+                if (b, h) == (BLOCKS - 1, PIECES - 1):
+                    nc.vector.tensor_scalar(x[b, h][:], picked[:], SCALE, None, ALU.mult)
+                else:
+                    nc.scalar.activation(x[b, h][:], picked[:], FUNC.Copy, scale=SCALE)
+
+        acc = {}
+        for kb in range(BLOCKS):
+            for h in range(PIECES):
+                for mb in range(BLOCKS):
+                    if kb == 0:
+                        acc[mb, h] = psum.tile([P, W], F32, name=f"acc{mb}_{h}")
+                    nc.tensor.matmul(
+                        acc[mb, h][:],
+                        weights[:, kb, mb * P : (mb + 1) * P],
+                        x[kb, h][:],
+                        start=(kb == 0),
+                        stop=(kb == BLOCKS - 1),
+                    )
+        for h in range(PIECES):
+            for mb in range(BLOCKS):
+                y = held.tile([P, W], F32, name=f"y{mb}_{h}")
+                nc.scalar.activation(y[:], acc[mb, h][:], FUNC.Gelu_apprx_tanh, bias=bias[:, mb : mb + 1])
+                nc.sync.dma_start(out[mb * P : (mb + 1) * P, h * W : (h + 1) * W], y[:])

@@ -63,12 +63,13 @@ def tile_sahp_kernel(tc, emb, seq_dt, wt, sin_arc, cos_arc, ws, bs, offs, out):
             return prod
 
         pe = [held.tile([P, N], F32, name=f"pe{b}") for b in range(BLOCKS)]
+        ss = held.tile([P, N], F32, name="ss")
+        nc.gpsimd.tensor_tensor(ss[:], sin_a[:], sin_p[:], ALU.mult)
         sc = scaled_product("sc", sin_a, cos_p)
         cc = scaled_product("cc", cos_a, cos_p)
         cs = scaled_product("cs", cos_a, sin_p)
-        ss = scaled_product("ss", sin_a, sin_p)
         nc.vector.tensor_tensor(pe[0][:], sc[:], cs[:], ALU.add)
-        nc.vector.tensor_tensor(pe[1][:], cc[:], ss[:], ALU.subtract)
+        nc.vector.scalar_tensor_tensor(pe[1][:], ss[:], -1.0 / SCALE, cc[:], ALU.mult, ALU.add)
 
         x = {}
         for b in range(BLOCKS):

@@ -26,8 +26,8 @@ def tile_sahp_kernel(tc, emb, seq_dt, wt, sin_arc, cos_arc, ws, bs, offs, out):
         tc.tile_pool(name="held", bufs=1) as held,
         tc.psum_pool(name="psum", bufs=1) as psum,
     ):
-        dt_all = held.tile([P, N], F32, name="dt_all")
-        nc.sync.dma_start(dt_all[:], seq_dt.broadcast_to([P, N]))
+        dt_row = held.tile([1, N], F32, name="dt_row")
+        nc.sync.dma_start(dt_row[:], seq_dt)
         wt_col = held.tile([P, 1], F32, name="wt_col")
         nc.scalar.dma_start(wt_col[:], wt)
         offsets = held.tile([P, N // 16], U16, name="offsets")
@@ -51,11 +51,22 @@ def tile_sahp_kernel(tc, emb, seq_dt, wt, sin_arc, cos_arc, ws, bs, offs, out):
         nc.vector.memset(zero[:], 0.0)
         scratch = held.tile([P, 2], F32, name="scratch")
         nc.scalar.activation(scratch[:, 0:1], zero[:], FUNC.Sin)
+        ones_row = held.tile([1, P], F32, name="ones_row")
+        nc.vector.memset(ones_row[:], 1.0)
+        dt_all = []
+        for h in range(PIECES):
+            dt_h = psum.tile([P, W], F32, name=f"dt_all{h}")
+            nc.tensor.matmul(dt_h[:], ones_row[:], dt_row[:, h * W : (h + 1) * W], start=True, stop=True)
+            dt_all.append(dt_h)
         cos_p = held.tile([P, N], F32, name="cos_p")
-        nc.scalar.activation(cos_p[:], dt_all[:], FUNC.Sin, bias=math.pi / 2, scale=wt_col[:, 0:1])
         sin_p = held.tile([P, N], F32, name="sin_p")
-        nc.scalar.activation(sin_p[:], dt_all[:], FUNC.Sin, scale=wt_col[:, 0:1])
-        nc.scalar.activation(scratch[:, 1:2], sin_p[:, 0:1], FUNC.Gelu_apprx_tanh)
+        for h in range(PIECES):
+            nc.scalar.activation(
+                cos_p[:, h * W : (h + 1) * W], dt_all[h][:], FUNC.Sin, bias=math.pi / 2, scale=wt_col[:, 0:1]
+            )
+        for h in range(PIECES):
+            nc.scalar.activation(sin_p[:, h * W : (h + 1) * W], dt_all[h][:], FUNC.Sin, scale=wt_col[:, 0:1])
+        nc.scalar.activation(scratch[:, 1:2], sin_p[:, N - 1 : N], FUNC.Gelu_apprx_tanh)
 
         def scaled_product(name, arc, shift):
             prod = held.tile([P, N], F32, name=name)
@@ -63,13 +74,12 @@ def tile_sahp_kernel(tc, emb, seq_dt, wt, sin_arc, cos_arc, ws, bs, offs, out):
             return prod
 
         pe = [held.tile([P, N], F32, name=f"pe{b}") for b in range(BLOCKS)]
-        ss = held.tile([P, N], F32, name="ss")
-        nc.gpsimd.tensor_tensor(ss[:], sin_a[:], sin_p[:], ALU.mult)
         sc = scaled_product("sc", sin_a, cos_p)
         cc = scaled_product("cc", cos_a, cos_p)
         cs = scaled_product("cs", cos_a, sin_p)
+        ss = scaled_product("ss", sin_a, sin_p)
         nc.vector.tensor_tensor(pe[0][:], sc[:], cs[:], ALU.add)
-        nc.vector.scalar_tensor_tensor(pe[1][:], ss[:], -1.0 / SCALE, cc[:], ALU.mult, ALU.add)
+        nc.vector.tensor_tensor(pe[1][:], cc[:], ss[:], ALU.subtract)
 
         x = {}
         for b in range(BLOCKS):

@@ -51,35 +51,33 @@ def tile_sahp_kernel(tc, emb, seq_dt, wt, sin_arc, cos_arc, ws, bs, offs, out):
         nc.vector.memset(zero[:], 0.0)
         scratch = held.tile([P, 2], F32, name="scratch")
         nc.scalar.activation(scratch[:, 0:1], zero[:], FUNC.Sin)
+
         ones_row = held.tile([1, P], F32, name="ones_row")
         nc.vector.memset(ones_row[:], 1.0)
-        dt_all = []
-        for h in range(PIECES):
-            dt_h = psum.tile([P, W], F32, name=f"dt_all{h}")
-            nc.tensor.matmul(dt_h[:], ones_row[:], dt_row[:, h * W : (h + 1) * W], start=True, stop=True)
-            dt_all.append(dt_h)
-        cos_p = held.tile([P, N], F32, name="cos_p")
-        sin_p = held.tile([P, N], F32, name="sin_p")
-        for h in range(PIECES):
-            nc.scalar.activation(
-                cos_p[:, h * W : (h + 1) * W], dt_all[h][:], FUNC.Sin, bias=math.pi / 2, scale=wt_col[:, 0:1]
-            )
-        for h in range(PIECES):
-            nc.scalar.activation(sin_p[:, h * W : (h + 1) * W], dt_all[h][:], FUNC.Sin, scale=wt_col[:, 0:1])
-        nc.scalar.activation(scratch[:, 1:2], sin_p[:, N - 1 : N], FUNC.Gelu_apprx_tanh)
 
         def scaled_product(name, arc, shift):
-            prod = held.tile([P, N], F32, name=name)
-            nc.vector.scalar_tensor_tensor(prod[:], arc[:], 1.0 / SCALE, shift[:], ALU.mult, ALU.mult)
+            prod = held.tile([P, W], F32, name=name)
+            nc.vector.scalar_tensor_tensor(prod[:], arc, 1.0 / SCALE, shift[:], ALU.mult, ALU.mult)
             return prod
 
-        pe = [held.tile([P, N], F32, name=f"pe{b}") for b in range(BLOCKS)]
-        sc = scaled_product("sc", sin_a, cos_p)
-        cc = scaled_product("cc", cos_a, cos_p)
-        cs = scaled_product("cs", cos_a, sin_p)
-        ss = scaled_product("ss", sin_a, sin_p)
-        nc.vector.tensor_tensor(pe[0][:], sc[:], cs[:], ALU.add)
-        nc.vector.tensor_tensor(pe[1][:], cc[:], ss[:], ALU.subtract)
+        pe = {}
+        for h in range(PIECES):
+            cols = slice(h * W, (h + 1) * W)
+            dt_all = psum.tile([P, W], F32, name=f"dt_all{h}")
+            nc.tensor.matmul(dt_all[:], ones_row[:], dt_row[:, cols], start=True, stop=True)
+            cos_p = held.tile([P, W], F32, name=f"cos_p{h}")
+            nc.scalar.activation(cos_p[:], dt_all[:], FUNC.Sin, bias=math.pi / 2, scale=wt_col[:, 0:1])
+            sin_p = held.tile([P, W], F32, name=f"sin_p{h}")
+            nc.scalar.activation(sin_p[:], dt_all[:], FUNC.Sin, scale=wt_col[:, 0:1])
+            sc = scaled_product(f"sc{h}", sin_a[:, cols], cos_p)
+            cc = scaled_product(f"cc{h}", cos_a[:, cols], cos_p)
+            cs = scaled_product(f"cs{h}", cos_a[:, cols], sin_p)
+            ss = scaled_product(f"ss{h}", sin_a[:, cols], sin_p)
+            pe[0, h] = held.tile([P, W], F32, name=f"pe0_{h}")
+            nc.vector.tensor_tensor(pe[0, h][:], sc[:], cs[:], ALU.add)
+            pe[1, h] = held.tile([P, W], F32, name=f"pe1_{h}")
+            nc.vector.tensor_tensor(pe[1, h][:], cc[:], ss[:], ALU.subtract)
+        nc.scalar.activation(scratch[:, 1:2], sin_p[:, 0:1], FUNC.Gelu_apprx_tanh)
 
         x = {}
         for b in range(BLOCKS):
@@ -88,7 +86,7 @@ def tile_sahp_kernel(tc, emb, seq_dt, wt, sin_arc, cos_arc, ws, bs, offs, out):
                 nc.vector.tensor_tensor(
                     picked[:],
                     table[b][:].indirect(offsets[:, h * W // 16 : (h + 1) * W // 16]),
-                    pe[b][:, h * W : (h + 1) * W],
+                    pe[b, h][:],
                     ALU.add,
                 )
                 x[b, h] = held.tile([P, W], BF16, name=f"x{b}_{h}")

@@ -30,19 +30,19 @@ def tile_sahp_kernel(tc, emb, seq_dt, wt, sin_arc, cos_arc, ws, bs, offs, out):
         nc.sync.dma_start(dt_row[:], seq_dt)
         wt_col = held.tile([P, 1], F32, name="wt_col")
         nc.scalar.dma_start(wt_col[:], wt)
-        offsets = held.tile([P, N // 16], U16, name="offsets")
-        nc.sync.dma_start(offsets[:], offs)
         sin_a = held.tile([P, N], F32, name="sin_a")
         nc.sync.dma_start(sin_a[:], sin_arc)
         cos_a = held.tile([P, N], F32, name="cos_a")
-        nc.sync.dma_start(cos_a[:], cos_arc)
+        nc.scalar.dma_start(cos_a[:], cos_arc)
+        offsets = held.tile([P, N // 16], U16, name="offsets")
+        nc.sync.dma_start(offsets[:], offs)
         table = []
         for b in range(BLOCKS):
             table_b = held.tile([P, S], F32, name=f"table{b}")
             nc.sync.dma_start(table_b[:], emb[b * P : (b + 1) * P, :])
             table.append(table_b)
         weights = held.tile([P, BLOCKS, C], BF16, name="weights")
-        nc.sync.dma_start(weights[:], ws.rearrange("(kb p) m -> p kb m", p=P))
+        nc.scalar.dma_start(weights[:], ws.rearrange("(kb p) m -> p kb m", p=P))
         bias = held.tile([P, BLOCKS], F32, name="bias")
         with nc.allow_non_contiguous_dma(reason="256 biases, one to a partition"):
             nc.scalar.dma_start(bias[:], bs.rearrange("(mb p) o -> p (mb o)", p=P))
@@ -55,29 +55,35 @@ def tile_sahp_kernel(tc, emb, seq_dt, wt, sin_arc, cos_arc, ws, bs, offs, out):
         ones_row = held.tile([1, P], F32, name="ones_row")
         nc.vector.memset(ones_row[:], 1.0)
 
-        def scaled_product(name, arc, shift):
+        sum_a = held.tile([P, N], F32, name="sum_a")
+        nc.vector.tensor_tensor(sum_a[:], sin_a[:], cos_a[:], ALU.add)
+
+        def scaled_product(name, arc, factor, shift):
             prod = held.tile([P, W], F32, name=name)
-            nc.vector.scalar_tensor_tensor(prod[:], arc, 1.0 / SCALE, shift[:], ALU.mult, ALU.mult)
+            nc.vector.scalar_tensor_tensor(prod[:], arc, factor / SCALE, shift[:], ALU.mult, ALU.mult)
             return prod
+
+        def sine_of_phi_plus(name, dt_all, angle):
+            sine = held.tile([P, W], F32, name=name)
+            nc.scalar.activation(sine[:], dt_all[:], FUNC.Sin, bias=angle, scale=wt_col[:, 0:1])
+            return sine
 
         pe = {}
         for h in range(PIECES):
             cols = slice(h * W, (h + 1) * W)
             dt_all = psum.tile([P, W], F32, name=f"dt_all{h}")
             nc.tensor.matmul(dt_all[:], ones_row[:], dt_row[:, cols], start=True, stop=True)
-            cos_p = held.tile([P, W], F32, name=f"cos_p{h}")
-            nc.scalar.activation(cos_p[:], dt_all[:], FUNC.Sin, bias=math.pi / 2, scale=wt_col[:, 0:1])
-            sin_p = held.tile([P, W], F32, name=f"sin_p{h}")
-            nc.scalar.activation(sin_p[:], dt_all[:], FUNC.Sin, scale=wt_col[:, 0:1])
-            sc = scaled_product(f"sc{h}", sin_a[:, cols], cos_p)
-            cc = scaled_product(f"cc{h}", cos_a[:, cols], cos_p)
-            cs = scaled_product(f"cs{h}", cos_a[:, cols], sin_p)
-            ss = scaled_product(f"ss{h}", sin_a[:, cols], sin_p)
+            cos_p = sine_of_phi_plus(f"cos_p{h}", dt_all, math.pi / 2)
+            minus = sine_of_phi_plus(f"minus{h}", dt_all, -math.pi / 4)
+            plus = sine_of_phi_plus(f"plus{h}", dt_all, math.pi / 4)
+            k1 = scaled_product(f"k1_{h}", sum_a[:, cols], 1.0, cos_p)
+            k2 = scaled_product(f"k2_{h}", cos_a[:, cols], math.sqrt(2.0), minus)
+            k3 = scaled_product(f"k3_{h}", sin_a[:, cols], math.sqrt(2.0), plus)
             pe[0, h] = held.tile([P, W], F32, name=f"pe0_{h}")
-            nc.vector.tensor_tensor(pe[0, h][:], sc[:], cs[:], ALU.add)
+            nc.vector.tensor_tensor(pe[0, h][:], k1[:], k2[:], ALU.add)
             pe[1, h] = held.tile([P, W], F32, name=f"pe1_{h}")
-            nc.vector.tensor_tensor(pe[1, h][:], cc[:], ss[:], ALU.subtract)
-        nc.scalar.activation(scratch[:, 1:2], sin_p[:, 0:1], FUNC.Gelu_apprx_tanh)
+            nc.vector.tensor_tensor(pe[1, h][:], k1[:], k3[:], ALU.subtract)
+        nc.scalar.activation(scratch[:, 1:2], plus[:, 0:1], FUNC.Gelu_apprx_tanh)
 
         x = {}
         for b in range(BLOCKS):

@@ -28,8 +28,8 @@ def tile_sahp_kernel(tc, emb, seq_dt, wt, sin_arc, cos_arc, ws, bs, offs, out):
     ):
         dt_row = held.tile([1, N], F32, name="dt_row")
         nc.sync.dma_start(dt_row[:], seq_dt)
-        wt_col = held.tile([P, 1], F32, name="wt_col")
-        nc.scalar.dma_start(wt_col[:], wt)
+        wt_row = held.tile([1, P], F32, name="wt_row")
+        nc.scalar.dma_start(wt_row[:], wt.rearrange("p o -> o p"))
         sin_a = held.tile([P, N], F32, name="sin_a")
         nc.sync.dma_start(sin_a[:], sin_arc)
         cos_a = held.tile([P, N], F32, name="cos_a")
@@ -52,37 +52,34 @@ def tile_sahp_kernel(tc, emb, seq_dt, wt, sin_arc, cos_arc, ws, bs, offs, out):
         scratch = held.tile([P, 2], F32, name="scratch")
         nc.scalar.activation(scratch[:, 0:1], zero[:], FUNC.Sin)
 
-        ones_row = held.tile([1, P], F32, name="ones_row")
-        nc.vector.memset(ones_row[:], 1.0)
-
         sum_a = held.tile([P, N], F32, name="sum_a")
         nc.vector.tensor_tensor(sum_a[:], sin_a[:], cos_a[:], ALU.add)
 
-        def scaled_product(name, arc, factor, shift):
-            prod = held.tile([P, W], F32, name=name)
-            nc.vector.scalar_tensor_tensor(prod[:], arc, factor / SCALE, shift[:], ALU.mult, ALU.mult)
-            return prod
-
-        def sine_of_phi_plus(name, dt_all, angle):
+        def sine_of_phi_plus(name, phi, angle):
             sine = held.tile([P, W], F32, name=name)
-            nc.scalar.activation(sine[:], dt_all[:], FUNC.Sin, bias=angle, scale=wt_col[:, 0:1])
+            nc.scalar.activation(sine[:], phi[:], FUNC.Sin, bias=angle)
             return sine
 
-        pe = {}
+        def product_16th(name, arc, factor, sine):
+            prod = held.tile([P, W], F32, name=name)
+            nc.vector.scalar_tensor_tensor(prod[:], arc, factor / SCALE, sine[:], ALU.mult, ALU.mult)
+            return prod
+
+        pe_16th = {}
         for h in range(PIECES):
             cols = slice(h * W, (h + 1) * W)
-            dt_all = psum.tile([P, W], F32, name=f"dt_all{h}")
-            nc.tensor.matmul(dt_all[:], ones_row[:], dt_row[:, cols], start=True, stop=True)
-            cos_p = sine_of_phi_plus(f"cos_p{h}", dt_all, math.pi / 2)
-            minus = sine_of_phi_plus(f"minus{h}", dt_all, -math.pi / 4)
-            plus = sine_of_phi_plus(f"plus{h}", dt_all, math.pi / 4)
-            k1 = scaled_product(f"k1_{h}", sum_a[:, cols], 1.0, cos_p)
-            k2 = scaled_product(f"k2_{h}", cos_a[:, cols], math.sqrt(2.0), minus)
-            k3 = scaled_product(f"k3_{h}", sin_a[:, cols], math.sqrt(2.0), plus)
-            pe[0, h] = held.tile([P, W], F32, name=f"pe0_{h}")
-            nc.vector.tensor_tensor(pe[0, h][:], k1[:], k2[:], ALU.add)
-            pe[1, h] = held.tile([P, W], F32, name=f"pe1_{h}")
-            nc.vector.tensor_tensor(pe[1, h][:], k1[:], k3[:], ALU.subtract)
+            phi = psum.tile([P, W], F32, name=f"phi{h}")
+            nc.tensor.matmul(phi[:], wt_row[:], dt_row[:, cols], start=True, stop=True)
+            cos_p = sine_of_phi_plus(f"cos_p{h}", phi, math.pi / 2)
+            minus = sine_of_phi_plus(f"minus{h}", phi, -math.pi / 4)
+            plus = sine_of_phi_plus(f"plus{h}", phi, math.pi / 4)
+            k1 = product_16th(f"k1_{h}", sum_a[:, cols], 1.0, cos_p)
+            k2 = product_16th(f"k2_{h}", cos_a[:, cols], math.sqrt(2.0), minus)
+            k3 = product_16th(f"k3_{h}", sin_a[:, cols], math.sqrt(2.0), plus)
+            pe_16th[0, h] = held.tile([P, W], F32, name=f"pe0_{h}")
+            nc.vector.tensor_tensor(pe_16th[0, h][:], k1[:], k2[:], ALU.add)
+            pe_16th[1, h] = held.tile([P, W], F32, name=f"pe1_{h}")
+            nc.vector.tensor_tensor(pe_16th[1, h][:], k1[:], k3[:], ALU.subtract)
         nc.scalar.activation(scratch[:, 1:2], plus[:, 0:1], FUNC.Gelu_apprx_tanh)
 
         x = {}
@@ -92,7 +89,7 @@ def tile_sahp_kernel(tc, emb, seq_dt, wt, sin_arc, cos_arc, ws, bs, offs, out):
                 nc.vector.tensor_tensor(
                     picked[:],
                     table[b][:].indirect(offsets[:, h * W // 16 : (h + 1) * W // 16]),
-                    pe[b, h][:],
+                    pe_16th[b, h][:],
                     ALU.add,
                 )
                 x[b, h] = held.tile([P, W], BF16, name=f"x{b}_{h}")

@@ -41,11 +41,12 @@ def tile_sahp_kernel(tc, emb, seq_dt, wt, sin_arc, cos_arc, ws, bs, offs, out):
             table_b = held.tile([P, S], F32, name=f"table{b}")
             nc.sync.dma_start(table_b[:], emb[b * P : (b + 1) * P, :])
             table.append(table_b)
-        weights = held.tile([P, BLOCKS, C], BF16, name="weights")
-        nc.scalar.dma_start(weights[:], ws.rearrange("(kb p) m -> p kb m", p=P))
+        weights = [held.tile([P, C], BF16, name=f"weights{kb}") for kb in range(BLOCKS)]
+        nc.scalar.dma_start(weights[0][:], ws[0:P, :])
+        nc.sync.dma_start(weights[1][:], ws[P : 2 * P, :])
         bias = held.tile([P, BLOCKS], F32, name="bias")
         with nc.allow_non_contiguous_dma(reason="256 biases, one to a partition"):
-            nc.scalar.dma_start(bias[:], bs.rearrange("(mb p) o -> p (mb o)", p=P))
+            nc.sync.dma_start(bias[:], bs.rearrange("(mb p) o -> p (mb o)", p=P))
 
         zero = held.tile([P, 1], F32, name="zero")
         nc.vector.memset(zero[:], 0.0)
@@ -106,7 +107,7 @@ def tile_sahp_kernel(tc, emb, seq_dt, wt, sin_arc, cos_arc, ws, bs, offs, out):
                         acc[mb, h] = psum.tile([P, W], F32, name=f"acc{mb}_{h}")
                     nc.tensor.matmul(
                         acc[mb, h][:],
-                        weights[:, kb, mb * P : (mb + 1) * P],
+                        weights[kb][:, mb * P : (mb + 1) * P],
                         x[kb, h][:],
                         start=(kb == 0),
                         stop=(kb == BLOCKS - 1),

import math

import concourse.mybir as mybir

F32 = mybir.dt.float32
BF16 = mybir.dt.bfloat16
U16 = mybir.dt.uint16
FUNC = mybir.ActivationFunctionType
ALU = mybir.AluOpType

P = 128
C = 256
S = 2048
N = 512
BLOCKS = C // P
SCALE = 16.0
PIECES = 2
W = N // PIECES

FLOPS = 2 * C * C * N


def tile_sahp_kernel(tc, emb, seq_dt, wt, sin_arc, cos_arc, ws, bs, offs, out):
    nc = tc.nc
    with (
        tc.tile_pool(name="held", bufs=1) as held,
        tc.psum_pool(name="psum", bufs=1) as psum,
    ):
        dt_row = held.tile([1, N], F32, name="dt_row")
        nc.sync.dma_start(dt_row[:], seq_dt)
        wt_row = held.tile([1, P], F32, name="wt_row")
        nc.scalar.dma_start(wt_row[:], wt.rearrange("p o -> o p"))
        sin_a = held.tile([P, N], F32, name="sin_a")
        nc.sync.dma_start(sin_a[:], sin_arc)
        cos_a = held.tile([P, N], F32, name="cos_a")
        nc.scalar.dma_start(cos_a[:], cos_arc)
        offsets = held.tile([P, N // 16], U16, name="offsets")
        nc.sync.dma_start(offsets[:], offs)
        table = []
        for b in range(BLOCKS):
            table_b = held.tile([P, S], F32, name=f"table{b}")
            nc.sync.dma_start(table_b[:], emb[b * P : (b + 1) * P, :])
            table.append(table_b)
        weights = [held.tile([P, C], BF16, name=f"weights{kb}") for kb in range(BLOCKS)]
        nc.scalar.dma_start(weights[0][:], ws[0:P, :])
        nc.sync.dma_start(weights[1][:], ws[P : 2 * P, :])
        bias = held.tile([P, BLOCKS], F32, name="bias")
        with nc.allow_non_contiguous_dma(reason="256 biases, one to a partition"):
            nc.sync.dma_start(bias[:], bs.rearrange("(mb p) o -> p (mb o)", p=P))

        zero = held.tile([P, 1], F32, name="zero")
        nc.vector.memset(zero[:], 0.0)
        scratch = held.tile([P, 2], F32, name="scratch")
        nc.scalar.activation(scratch[:, 0:1], zero[:], FUNC.Sin)

        sum_a = held.tile([P, N], F32, name="sum_a")
        nc.vector.tensor_tensor(sum_a[:], sin_a[:], cos_a[:], ALU.add)

        def sine_of_phi_plus(name, phi, angle):
            sine = held.tile([P, W], F32, name=name)
            nc.scalar.activation(sine[:], phi[:], FUNC.Sin, bias=angle)
            return sine

        def product_16th(name, arc, factor, sine):
            prod = held.tile([P, W], F32, name=name)
            nc.vector.scalar_tensor_tensor(prod[:], arc, factor / SCALE, sine[:], ALU.mult, ALU.mult)
            return prod

        pe_16th = {}
        for h in range(PIECES):
            cols = slice(h * W, (h + 1) * W)
            phi = psum.tile([P, W], F32, name=f"phi{h}")
            nc.tensor.matmul(phi[:], wt_row[:], dt_row[:, cols], start=True, stop=True)
            cos_p = sine_of_phi_plus(f"cos_p{h}", phi, math.pi / 2)
            minus = sine_of_phi_plus(f"minus{h}", phi, -math.pi / 4)
            plus = sine_of_phi_plus(f"plus{h}", phi, math.pi / 4)
            k1 = product_16th(f"k1_{h}", sum_a[:, cols], 1.0, cos_p)
            k2 = product_16th(f"k2_{h}", cos_a[:, cols], math.sqrt(2.0), minus)
            k3 = product_16th(f"k3_{h}", sin_a[:, cols], math.sqrt(2.0), plus)
            pe_16th[0, h] = held.tile([P, W], F32, name=f"pe0_{h}")
            nc.vector.tensor_tensor(pe_16th[0, h][:], k1[:], k2[:], ALU.add)
            pe_16th[1, h] = held.tile([P, W], F32, name=f"pe1_{h}")
            nc.vector.tensor_tensor(pe_16th[1, h][:], k1[:], k3[:], ALU.subtract)
        nc.scalar.activation(scratch[:, 1:2], plus[:, 0:1], FUNC.Gelu_apprx_tanh)

        x = {}
        for b in range(BLOCKS):
            for h in range(PIECES):
                picked = held.tile([P, W], F32, name=f"picked{b}_{h}")
                nc.vector.tensor_tensor(
                    picked[:],
                    table[b][:].indirect(offsets[:, h * W // 16 : (h + 1) * W // 16]),
                    pe_16th[b, h][:],
                    ALU.add,
                )
                x[b, h] = held.tile([P, W], BF16, name=f"x{b}_{h}")
                if (b, h) == (BLOCKS - 1, PIECES - 1):
                    nc.vector.tensor_scalar(x[b, h][:], picked[:], SCALE, None, ALU.mult)
                else:
                    nc.scalar.activation(x[b, h][:], picked[:], FUNC.Copy, scale=SCALE)

        acc = {}
        for kb in range(BLOCKS):
            for h in range(PIECES):
                for mb in range(BLOCKS):
                    if kb == 0:
                        acc[mb, h] = psum.tile([P, W], F32, name=f"acc{mb}_{h}")
                    nc.tensor.matmul(
                        acc[mb, h][:],
                        weights[kb][:, mb * P : (mb + 1) * P],
                        x[kb, h][:],
                        start=(kb == 0),
                        stop=(kb == BLOCKS - 1),
                    )
        for h in range(PIECES):
            for mb in range(BLOCKS):
                y = held.tile([P, W], F32, name=f"y{mb}_{h}")
                nc.scalar.activation(y[:], acc[mb, h][:], FUNC.Gelu_apprx_tanh, bias=bias[:, mb : mb + 1])
                nc.sync.dma_start(out[mb * P : (mb + 1) * P, h * W : (h + 1) * W], y[:])
